import numpy as np
import ml_dtypes


def mxq(x, axis, fmt="e4m3"):
    dtype, down = {"e4m3": (ml_dtypes.float8_e4m3fn, 7), "e5m2": (ml_dtypes.float8_e5m2, 14)}[fmt]
    v = np.moveaxis(np.asarray(x, np.float32).astype(ml_dtypes.bfloat16).astype(np.float64), axis, -1)
    blocks = v.reshape(v.shape[:-1] + (-1, 32))
    amax = np.abs(blocks).max(-1, keepdims=True)
    byte = np.maximum(np.where(amax > 0, np.frexp(amax)[1] - 1 + 127, 0) - down, 1)
    scale = np.exp2(byte - 127.0)
    codes = (blocks / scale).astype(np.float32).astype(dtype).astype(np.float64)
    return np.moveaxis((codes * scale).reshape(v.shape), -1, axis)


WIDE = False


def mx_kscale(k):
    if not WIDE:
        return np.ones(k)
    levels = np.array([10, -10, 5, -5, 0])
    a = np.random.permutation(np.resize(levels, k // 512 * 4)).reshape(k // 512, 4)
    idx = np.arange(k)
    return np.exp2(a[idx // 512, idx % 128 // 32])


BF16 = ml_dtypes.bfloat16


def bf(x):
    return np.asarray(x, np.float32).astype(BF16)


def f64(x):
    return np.asarray(x).astype(np.float64)


E2M1 = np.array([0.0, 0.5, 1.0, 1.5, 2.0, 3.0, 4.0, 6.0, -0.0, -0.5, -1.0, -1.5, -2.0, -3.0, -4.0, -6.0])


def pack_weight(w, fmt):
    k, n = w.shape
    w = f64(bf(w)).reshape(k // 32, 32, n)
    amax = np.abs(w).max(1)
    if fmt == "e4m3":
        byte = np.frexp(amax)[1] - 1 + 127 - 7
    else:
        mant, ex = np.frexp(amax / 6.0)
        byte = np.where(mant > 0.5, ex, ex - 1) + 127
    byte = np.clip(np.where(amax > 0, byte, 1), 1, 254)
    scaled = (w * np.exp2(127.0 - byte)[:, None, :]).reshape(k, n).astype(np.float32)
    by_word = np.ascontiguousarray(scaled.reshape(k // 512, 128, 4, n).transpose(0, 1, 3, 2))
    if fmt == "e4m3":
        words = by_word.astype(ml_dtypes.float8_e4m3fn).view(np.uint8)
    else:
        c = by_word.astype(ml_dtypes.float4_e2m1fn).view(np.uint8) & 0xF
        words = c[..., 0::2] | (c[..., 1::2] << 4)
    return np.ascontiguousarray(words), np.ascontiguousarray(byte.astype(np.uint8).reshape(k // 512, 16, n))


def unpack_weight(words, scales, fmt):
    g, p, n, _ = words.shape
    if fmt == "e4m3":
        vals = np.ascontiguousarray(words).view(ml_dtypes.float8_e4m3fn).astype(np.float64)
    else:
        nib = np.empty((g, p, n, 4), np.uint8)
        nib[..., 0::2] = words & 0xF
        nib[..., 1::2] = words >> 4
        vals = E2M1[nib]
    vals = vals * np.repeat(np.exp2(scales.astype(np.float64) - 127.0), 8, axis=1)[..., None]
    return vals.transpose(0, 1, 3, 2).reshape(g * 512, n)


B, F, E, H, D0, D1 = 4096, 8, 128, 128, 64, 128
FH = F * H


def setup_inputs():
    t = mx_kscale(FH)
    tf = t.reshape(F, H)
    x = bf(np.random.standard_normal((B, F, E)))
    feat_w = bf(np.random.standard_normal((F, E, H)) / np.sqrt(E) * tf[:, None, :])
    feat_b = bf(np.random.standard_normal((F, H)) * 0.2 * tf)
    trans_w_words, trans_w_scales = pack_weight(np.random.standard_normal((FH, FH)) / np.sqrt(FH) / t[:, None] * t[None, :], "e4m3")
    trans_b = bf(np.random.standard_normal(FH) * 0.2 * t)
    return {"x": x,
            "feat_w": feat_w,
            "feat_b": feat_b,
            "trans_w_words": trans_w_words,
            "trans_w_scales": trans_w_scales,
            "trans_b": trans_b}


def reference(x, feat_w, feat_b, trans_w_words, trans_w_scales, trans_b):
    pre = (f64(x).transpose(1, 0, 2) @ f64(feat_w)).transpose(1, 0, 2) + f64(feat_b)
    h = np.maximum(pre, 0.0)
    hf = h.reshape(B, FH)
    return np.maximum((mxq(hf, 1, "e4m3") @ unpack_weight(trans_w_words, trans_w_scales, "e4m3")) + f64(trans_b), 0.0) + hf

@@ -1,0 +1,179 @@
+from contextlib import ExitStack
+
+import concourse.mybir as mybir
+from concourse.masks import make_identity
+
+FP8X4 = mybir.dt.float8_e4m3fn_x4
+BF16 = mybir.dt.bfloat16
+F32 = mybir.dt.float32
+I32 = mybir.dt.int32
+U32 = mybir.dt.uint32
+U8 = mybir.dt.uint8
+ADD = mybir.AluOpType.add
+MAX = mybir.AluOpType.max
+MIN = mybir.AluOpType.min
+RELU = mybir.ActivationFunctionType.Relu
+
+P = 128
+B, F, E, H = 4096, 8, 128, 128
+FH = F * H
+K_PASS = 4 * P
+PASSES = FH // K_PASS
+F_PASS = K_PASS // H
+BANK = 512
+HALVES = FH // BANK
+TILES = B // P
+X_AHEAD = 4
+
+FLOPS = 2 * B * (F * E * H + FH * FH)
+
+
+def tile_dsfs_pa_t_kernel(tc, x, feat_w, feat_b, trans_w_words, trans_w_scales, trans_b, out):
+    nc = tc.nc
+    x_rows = x.rearrange("(i p) f e -> i p (f e)", p=P)
+    out_rows = out.rearrange("(i p) n -> i p n", p=P)
+
+    with ExitStack() as stack:
+        consts = stack.enter_context(tc.tile_pool(name="consts", bufs=1))
+        x_pool = stack.enter_context(tc.tile_pool(name="x_pool", bufs=X_AHEAD + 2))
+        xt_pool = stack.enter_context(tc.tile_pool(name="xt_pool", bufs=2))
+        h_pool = stack.enter_context(tc.tile_pool(name="h_pool", bufs=5))
+        hb_pool = stack.enter_context(tc.tile_pool(name="hb_pool", bufs=2))
+        q_pool = stack.enter_context(tc.tile_pool(name="q_pool", bufs=2))
+        o_pool = stack.enter_context(tc.tile_pool(name="o_pool", bufs=4))
+        xt_psum = stack.enter_context(tc.psum_pool(name="xt_psum", bufs=2))
+        pre_psum = stack.enter_context(tc.psum_pool(name="pre_psum", bufs=2))
+        ht_psum = stack.enter_context(tc.psum_pool(name="ht_psum", bufs=2))
+        acc_psum = stack.enter_context(tc.psum_pool(name="acc_psum", bufs=2))
+
+        x_tiles = {}
+        xt_tiles = {}
+        h_tiles = {}
+        hb_tiles = {}
+        code_tiles = {}
+
+        def load_x(i):
+            x_sb = x_pool.tile([P, FH], BF16)
+            nc.sync.dma_start(out=x_sb[:], in_=x_rows[i])
+            x_tiles[i] = x_sb
+
+        ident_bf = consts.tile([P, P], BF16)
+        make_identity(nc, ident_bf[:])
+        ident_f32 = consts.tile([P, P], F32)
+        make_identity(nc, ident_f32[:])
+
+        w_scales = consts.tile([P, PASSES, FH], U8, align_bytes=64)
+        nc.vector.memset(w_scales[:].bitcast(I32), 0)
+
+        load_x(0)
+        fw = consts.tile([P, F, H], BF16)
+        nc.sync.dma_start(out=fw[:], in_=feat_w.rearrange("f e h -> e f h"))
+        fb = consts.tile([P, FH], BF16)
+        nc.sync.dma_start(out=fb[:], in_=feat_b.rearrange("f h -> (f h)").partition_broadcast(P))
+        load_x(1)
+        for quad in range(4):
+            nc.sync.dma_start(
+                out=w_scales[32 * quad : 32 * quad + 4, :, :].bitcast(I32),
+                in_=trans_w_scales[:, 4 * quad : 4 * quad + 4, :].rearrange("g r n -> r g n").bitcast(I32),
+            )
+        w_codes = consts.tile([P, PASSES, FH], U32, align_bytes=64)
+        for g in range(PASSES):
+            nc.sync.dma_start(
+                out=w_codes[:, g, :].bitcast(I32),
+                in_=trans_w_words[g].rearrange("p n t -> p (n t)").bitcast(I32),
+            )
+        tb = consts.tile([P, FH], BF16)
+        nc.sync.dma_start(out=tb[:], in_=trans_b.partition_broadcast(P))
+        for i in range(2, X_AHEAD):
+            load_x(i)
+
+        def transpose_x(i):
+            xt_ps = xt_psum.tile([P, F, P], BF16)
+            for f in range(F):
+                nc.tensor.transpose(xt_ps[:, f, :], x_tiles[i][:, f * E : (f + 1) * E], ident_bf[:])
+            xt = xt_pool.tile([P, F, P], BF16)
+            nc.scalar.copy(out=xt[:], in_=xt_ps[:])
+            xt_tiles[i] = xt
+
+        def feature_layers(i):
+            h = h_pool.tile([P, FH], F32)
+            hb = hb_pool.tile([P, PASSES, K_PASS], BF16)
+            for g in range(PASSES):
+                cols = slice(g * K_PASS, (g + 1) * K_PASS)
+                pre_ps = pre_psum.tile([P, K_PASS], F32)
+                for j in range(F_PASS):
+                    f = g * F_PASS + j
+                    nc.tensor.matmul(
+                        pre_ps[:, j * H : (j + 1) * H], lhsT=xt_tiles[i][:, f, :], rhs=fw[:, f, :], start=True, stop=True
+                    )
+                nc.vector.tensor_tensor(out=h[:, cols], in0=pre_ps[:], in1=fb[:, cols], op=ADD)
+                nc.scalar.activation(
+                    out=hb[:, g, :].rearrange("p (u q e) -> p u q e", u=2, e=2),
+                    in_=h[:, cols].rearrange("p (q u e) -> p u q e", u=2, e=2),
+                    func=RELU,
+                )
+            nc.gpsimd.tensor_scalar(out=h[:], in0=h[:], scalar1=float("inf"), scalar2=0.0, op0=MIN, op1=MAX)
+            h_tiles[i] = h
+            hb_tiles[i] = hb
+
+        def quantise_h(i):
+            ht_ps = ht_psum.tile([P, PASSES, 2, P], F32)
+            hb_words = hb_tiles[i][:].bitcast(F32)
+            for g in range(PASSES):
+                for u in range(2):
+                    nc.tensor.transpose(ht_ps[:, g, u, :], hb_words[:, g, u * P : (u + 1) * P], ident_f32[:])
+            grouped = q_pool.tile([P, PASSES, K_PASS], BF16, align_bytes=64)
+            nc.scalar.copy(
+                out=grouped[:].bitcast(F32).rearrange("p g (r u) -> p g r u", u=2),
+                in_=ht_ps[:].rearrange("p g u r -> p g r u"),
+            )
+            h_codes = q_pool.tile([P, PASSES * P], U32, align_bytes=64)
+            h_scales = q_pool.tile([P, PASSES * P], U8, align_bytes=64)
+            code_tiles[i] = (grouped, h_codes, h_scales)
+
+        def quantise_h_2(i):
+            grouped, h_codes, h_scales = code_tiles[i]
+            nc.vector.quantize_mx(
+                out=h_codes[:].bitcast(FP8X4), scales=h_scales[:], in_=grouped[:].rearrange("p g c -> p (g c)")
+            )
+
+        def second_layer(i):
+            grouped, h_codes, h_scales = code_tiles[i]
+            h = h_tiles[i]
+            o = o_pool.tile([P, FH], F32)
+            for half in range(HALVES):
+                cols = slice(half * BANK, (half + 1) * BANK)
+                acc = acc_psum.tile([P, BANK], F32)
+                for g in range(PASSES):
+                    rows = slice(g * P, (g + 1) * P)
+                    nc.tensor.matmul_mx(
+                        out=acc[:],
+                        lhsT=h_codes[:, rows].bitcast(FP8X4),
+                        lhsT_scale=h_scales[:, rows],
+                        rhs=w_codes[:, g, cols].bitcast(FP8X4),
+                        rhs_scale=w_scales[:, g, cols],
+                        start=(g == 0),
+                        stop=(g == PASSES - 1),
+                    )
+                nc.vector.tensor_tensor(out=o[:, cols], in0=acc[:], in1=tb[:, cols], op=ADD)
+            left = slice(0, BANK)
+            right = slice(BANK, FH)
+            nc.scalar.activation(out=o[:, left], in_=o[:, left], func=RELU)
+            nc.gpsimd.tensor_tensor(out=o[:, left], in0=o[:, left], in1=h[:, left], op=ADD)
+            nc.vector.scalar_tensor_tensor(out=o[:, right], in0=o[:, right], scalar=0.0, in1=h[:, right], op0=MAX, op1=ADD)
+            nc.sync.dma_start(out=out_rows[i], in_=o[:])
+
+        stack.enter_context(tc.manual_schedule())
+        for step in range(TILES + 3):
+            if step + X_AHEAD < TILES:
+                load_x(step + X_AHEAD)
+            if step < TILES:
+                transpose_x(step)
+            if 0 <= step - 2 < TILES:
+                quantise_h(step - 2)
+            if 0 <= step - 1 < TILES:
+                feature_layers(step - 1)
+            if 0 <= step - 2 < TILES:
+                quantise_h_2(step - 2)
+            if 0 <= step - 3 < TILES:
+                second_layer(step - 3)

@@ -11,7 +11,6 @@ U32 = mybir.dt.uint32
 U8 = mybir.dt.uint8
 ADD = mybir.AluOpType.add
 MAX = mybir.AluOpType.max
-MIN = mybir.AluOpType.min
 RELU = mybir.ActivationFunctionType.Relu
 
 P = 128
@@ -112,7 +111,7 @@ def tile_dsfs_pa_t_kernel(tc, x, feat_w, feat_b, trans_w_words, trans_w_scales, 
                     in_=h[:, cols].rearrange("p (q u e) -> p u q e", u=2, e=2),
                     func=RELU,
                 )
-            nc.gpsimd.tensor_scalar(out=h[:], in0=h[:], scalar1=float("inf"), scalar2=0.0, op0=MIN, op1=MAX)
+            nc.scalar.activation(out=h[:], in_=h[:], func=RELU)
             h_tiles[i] = h
             hb_tiles[i] = hb
 
@@ -156,11 +155,7 @@ def tile_dsfs_pa_t_kernel(tc, x, feat_w, feat_b, trans_w_words, trans_w_scales, 
                         stop=(g == PASSES - 1),
                     )
                 nc.vector.tensor_tensor(out=o[:, cols], in0=acc[:], in1=tb[:, cols], op=ADD)
-            left = slice(0, BANK)
-            right = slice(BANK, FH)
-            nc.scalar.activation(out=o[:, left], in_=o[:, left], func=RELU)
-            nc.gpsimd.tensor_tensor(out=o[:, left], in0=o[:, left], in1=h[:, left], op=ADD)
-            nc.vector.scalar_tensor_tensor(out=o[:, right], in0=o[:, right], scalar=0.0, in1=h[:, right], op0=MAX, op1=ADD)
+            nc.vector.scalar_tensor_tensor(out=o[:], in0=o[:], scalar=0.0, in1=h[:], op0=MAX, op1=ADD)
             nc.sync.dma_start(out=out_rows[i], in_=o[:])
 
         stack.enter_context(tc.manual_schedule())

@@ -11,6 +11,7 @@ U32 = mybir.dt.uint32
 U8 = mybir.dt.uint8
 ADD = mybir.AluOpType.add
 MAX = mybir.AluOpType.max
+MIN = mybir.AluOpType.min
 RELU = mybir.ActivationFunctionType.Relu
 
 P = 128
@@ -36,9 +37,9 @@ def tile_dsfs_pa_t_kernel(tc, x, feat_w, feat_b, trans_w_words, trans_w_scales, 
         consts = stack.enter_context(tc.tile_pool(name="consts", bufs=1))
         x_pool = stack.enter_context(tc.tile_pool(name="x_pool", bufs=X_AHEAD + 2))
         xt_pool = stack.enter_context(tc.tile_pool(name="xt_pool", bufs=2))
-        h_pool = stack.enter_context(tc.tile_pool(name="h_pool", bufs=5))
+        h_pool = stack.enter_context(tc.tile_pool(name="h_pool", bufs=6))
         hb_pool = stack.enter_context(tc.tile_pool(name="hb_pool", bufs=2))
-        q_pool = stack.enter_context(tc.tile_pool(name="q_pool", bufs=2))
+        q_pool = stack.enter_context(tc.tile_pool(name="q_pool", bufs=3))
         o_pool = stack.enter_context(tc.tile_pool(name="o_pool", bufs=4))
         xt_psum = stack.enter_context(tc.psum_pool(name="xt_psum", bufs=2))
         pre_psum = stack.enter_context(tc.psum_pool(name="pre_psum", bufs=2))
@@ -50,6 +51,7 @@ def tile_dsfs_pa_t_kernel(tc, x, feat_w, feat_b, trans_w_words, trans_w_scales, 
         h_tiles = {}
         hb_tiles = {}
         code_tiles = {}
+        o_tiles = {}
 
         def load_x(i):
             x_sb = x_pool.tile([P, FH], BF16)
@@ -99,21 +101,38 @@ def tile_dsfs_pa_t_kernel(tc, x, feat_w, feat_b, trans_w_words, trans_w_scales, 
             hb = hb_pool.tile([P, PASSES, K_PASS], BF16)
             for g in range(PASSES):
                 cols = slice(g * K_PASS, (g + 1) * K_PASS)
+                bias_on_tensor = g == 0
                 pre_ps = pre_psum.tile([P, K_PASS], F32)
+                if bias_on_tensor:
+                    nc.tensor.matmul(pre_ps[:], lhsT=ident_bf[:], rhs=fb[:, cols], start=True, stop=False)
                 for j in range(F_PASS):
                     f = g * F_PASS + j
                     nc.tensor.matmul(
-                        pre_ps[:, j * H : (j + 1) * H], lhsT=xt_tiles[i][:, f, :], rhs=fw[:, f, :], start=True, stop=True
+                        pre_ps[:, j * H : (j + 1) * H],
+                        lhsT=xt_tiles[i][:, f, :],
+                        rhs=fw[:, f, :],
+                        start=not bias_on_tensor,
+                        stop=(not bias_on_tensor) or j == F_PASS - 1,
                     )
-                nc.vector.tensor_tensor(out=h[:, cols], in0=pre_ps[:], in1=fb[:, cols], op=ADD)
+                if bias_on_tensor:
+                    biased = pre_ps[:]
+                else:
+                    nc.vector.tensor_tensor(out=h[:, cols], in0=pre_ps[:], in1=fb[:, cols], op=ADD)
+                    biased = h[:, cols]
                 nc.scalar.activation(
                     out=hb[:, g, :].rearrange("p (u q e) -> p u q e", u=2, e=2),
-                    in_=h[:, cols].rearrange("p (q u e) -> p u q e", u=2, e=2),
+                    in_=biased.rearrange("p (q u e) -> p u q e", u=2, e=2),
                     func=RELU,
                 )
-            nc.scalar.activation(out=h[:], in_=h[:], func=RELU)
+                if bias_on_tensor:
+                    nc.scalar.activation(out=h[:, cols], in_=biased, func=RELU)
             h_tiles[i] = h
             hb_tiles[i] = hb
+
+        def relu_of_vector_half(i):
+            cols = slice(K_PASS, FH)
+            h = h_tiles[i]
+            nc.gpsimd.tensor_scalar(out=h[:, cols], in0=h[:, cols], scalar1=float("inf"), scalar2=0.0, op0=MIN, op1=MAX)
 
         def quantise_h(i):
             ht_ps = ht_psum.tile([P, PASSES, 2, P], F32)
@@ -138,7 +157,6 @@ def tile_dsfs_pa_t_kernel(tc, x, feat_w, feat_b, trans_w_words, trans_w_scales, 
 
         def second_layer(i):
             grouped, h_codes, h_scales = code_tiles[i]
-            h = h_tiles[i]
             o = o_pool.tile([P, FH], F32)
             for half in range(HALVES):
                 cols = slice(half * BANK, (half + 1) * BANK)
@@ -155,20 +173,27 @@ def tile_dsfs_pa_t_kernel(tc, x, feat_w, feat_b, trans_w_words, trans_w_scales, 
                         stop=(g == PASSES - 1),
                     )
                 nc.vector.tensor_tensor(out=o[:, cols], in0=acc[:], in1=tb[:, cols], op=ADD)
-            nc.vector.scalar_tensor_tensor(out=o[:], in0=o[:], scalar=0.0, in1=h[:], op0=MAX, op1=ADD)
+            o_tiles[i] = o
+
+        def finish(i):
+            o = o_tiles[i]
+            nc.vector.scalar_tensor_tensor(out=o[:], in0=o[:], scalar=0.0, in1=h_tiles[i][:], op0=MAX, op1=ADD)
             nc.sync.dma_start(out=out_rows[i], in_=o[:])
 
-        stack.enter_context(tc.manual_schedule())
-        for step in range(TILES + 3):
+        for step in range(TILES + 4):
             if step + X_AHEAD < TILES:
                 load_x(step + X_AHEAD)
+            if 0 <= step - 3 < TILES:
+                quantise_h_2(step - 3)
+            if 0 <= step - 4 < TILES:
+                finish(step - 4)
+            if 0 <= step - 1 < TILES:
+                feature_layers(step - 1)
             if step < TILES:
                 transpose_x(step)
             if 0 <= step - 2 < TILES:
                 quantise_h(step - 2)
             if 0 <= step - 1 < TILES:
-                feature_layers(step - 1)
-            if 0 <= step - 2 < TILES:
-                quantise_h_2(step - 2)
+                relu_of_vector_half(step - 1)
             if 0 <= step - 3 < TILES:
                 second_layer(step - 3)

@@ -11,7 +11,6 @@ U32 = mybir.dt.uint32
 U8 = mybir.dt.uint8
 ADD = mybir.AluOpType.add
 MAX = mybir.AluOpType.max
-MIN = mybir.AluOpType.min
 RELU = mybir.ActivationFunctionType.Relu
 
 P = 128
@@ -132,7 +131,7 @@ def tile_dsfs_pa_t_kernel(tc, x, feat_w, feat_b, trans_w_words, trans_w_scales, 
         def relu_of_vector_half(i):
             cols = slice(K_PASS, FH)
             h = h_tiles[i]
-            nc.gpsimd.tensor_scalar(out=h[:, cols], in0=h[:, cols], scalar1=float("inf"), scalar2=0.0, op0=MIN, op1=MAX)
+            nc.scalar.activation(out=h[:, cols], in_=h[:, cols], func=RELU)
 
         def quantise_h(i):
             ht_ps = ht_psum.tile([P, PASSES, 2, P], F32)

@@ -11,6 +11,7 @@ U32 = mybir.dt.uint32
 U8 = mybir.dt.uint8
 ADD = mybir.AluOpType.add
 MAX = mybir.AluOpType.max
+MIN = mybir.AluOpType.min
 RELU = mybir.ActivationFunctionType.Relu
 
 P = 128
@@ -35,9 +36,9 @@ def tile_dsfs_pa_t_kernel(tc, x, feat_w, feat_b, trans_w_words, trans_w_scales, 
     with ExitStack() as stack:
         consts = stack.enter_context(tc.tile_pool(name="consts", bufs=1))
         x_pool = stack.enter_context(tc.tile_pool(name="x_pool", bufs=X_AHEAD + 2))
-        xt_pool = stack.enter_context(tc.tile_pool(name="xt_pool", bufs=2))
-        h_pool = stack.enter_context(tc.tile_pool(name="h_pool", bufs=6))
-        hb_pool = stack.enter_context(tc.tile_pool(name="hb_pool", bufs=2))
+        xt_pool = stack.enter_context(tc.tile_pool(name="xt_pool", bufs=3))
+        h_pool = stack.enter_context(tc.tile_pool(name="h_pool", bufs=7))
+        hb_pool = stack.enter_context(tc.tile_pool(name="hb_pool", bufs=3))
         q_pool = stack.enter_context(tc.tile_pool(name="q_pool", bufs=3))
         o_pool = stack.enter_context(tc.tile_pool(name="o_pool", bufs=4))
         xt_psum = stack.enter_context(tc.psum_pool(name="xt_psum", bufs=2))
@@ -97,48 +98,39 @@ def tile_dsfs_pa_t_kernel(tc, x, feat_w, feat_b, trans_w_words, trans_w_scales, 
 
         def feature_layers(i):
             h = h_pool.tile([P, FH], F32)
-            hb = hb_pool.tile([P, PASSES, K_PASS], BF16)
-            for g in range(PASSES):
-                cols = slice(g * K_PASS, (g + 1) * K_PASS)
-                bias_on_tensor = g == 0
-                pre_ps = pre_psum.tile([P, K_PASS], F32)
-                if bias_on_tensor:
-                    nc.tensor.matmul(pre_ps[:], lhsT=ident_bf[:], rhs=fb[:, cols], start=True, stop=False)
-                for j in range(F_PASS):
-                    f = g * F_PASS + j
-                    nc.tensor.matmul(
-                        pre_ps[:, j * H : (j + 1) * H],
-                        lhsT=xt_tiles[i][:, f, :],
-                        rhs=fw[:, f, :],
-                        start=not bias_on_tensor,
-                        stop=(not bias_on_tensor) or j == F_PASS - 1,
-                    )
-                if bias_on_tensor:
-                    biased = pre_ps[:]
-                else:
-                    nc.vector.tensor_tensor(out=h[:, cols], in0=pre_ps[:], in1=fb[:, cols], op=ADD)
-                    biased = h[:, cols]
-                nc.scalar.activation(
-                    out=hb[:, g, :].rearrange("p (u q e) -> p u q e", u=2, e=2),
-                    in_=biased.rearrange("p (q u e) -> p u q e", u=2, e=2),
-                    func=RELU,
-                )
-                if bias_on_tensor:
-                    nc.scalar.activation(out=h[:, cols], in_=biased, func=RELU)
             h_tiles[i] = h
+            left = slice(0, K_PASS)
+            right = slice(K_PASS, FH)
+            pre_left = pre_psum.tile([P, K_PASS], F32, name="pre_ps")
+            nc.tensor.matmul(pre_left[:], lhsT=ident_bf[:], rhs=fb[:, left], start=True, stop=False)
+            for f in range(F_PASS):
+                nc.tensor.matmul(
+                    pre_left[:, f * H : (f + 1) * H], lhsT=xt_tiles[i][:, f, :], rhs=fw[:, f, :], start=False, stop=(f == F_PASS - 1)
+                )
+            nc.scalar.activation(out=h[:, left], in_=pre_left[:], func=RELU)
+            pre_right = pre_psum.tile([P, K_PASS], F32, name="pre_ps")
+            for f in range(F_PASS, F):
+                nc.tensor.matmul(
+                    pre_right[:, (f - F_PASS) * H : (f - F_PASS + 1) * H], lhsT=xt_tiles[i][:, f, :], rhs=fw[:, f, :], start=True, stop=True
+                )
+            nc.vector.tensor_tensor(out=h[:, right], in0=pre_right[:], in1=fb[:, right], op=ADD)
+
+        def round_h(i):
+            hb = hb_pool.tile([P, 2, FH // 4, 2], BF16)
+            nc.scalar.activation(out=hb[:], in_=h_tiles[i][:].rearrange("p (c u e) -> p u c e", u=2, e=2), func=RELU)
             hb_tiles[i] = hb
 
         def relu_of_vector_half(i):
             cols = slice(K_PASS, FH)
             h = h_tiles[i]
-            nc.scalar.activation(out=h[:, cols], in_=h[:, cols], func=RELU)
+            nc.gpsimd.tensor_scalar(out=h[:, cols], in0=h[:, cols], scalar1=float("inf"), scalar2=0.0, op0=MIN, op1=MAX)
 
         def quantise_h(i):
             ht_ps = ht_psum.tile([P, PASSES, 2, P], F32)
-            hb_words = hb_tiles[i][:].bitcast(F32)
+            hb_words = hb_tiles[i][:].rearrange("p u c e -> p u (c e)").bitcast(F32)
             for g in range(PASSES):
                 for u in range(2):
-                    nc.tensor.transpose(ht_ps[:, g, u, :], hb_words[:, g, u * P : (u + 1) * P], ident_f32[:])
+                    nc.tensor.transpose(ht_ps[:, g, u, :], hb_words[:, u, g * P : (g + 1) * P], ident_f32[:])
             grouped = q_pool.tile([P, PASSES, K_PASS], BF16, align_bytes=64)
             nc.scalar.copy(
                 out=grouped[:].bitcast(F32).rearrange("p g (r u) -> p g r u", u=2),
@@ -179,20 +171,23 @@ def tile_dsfs_pa_t_kernel(tc, x, feat_w, feat_b, trans_w_words, trans_w_scales, 
             nc.vector.scalar_tensor_tensor(out=o[:], in0=o[:], scalar=0.0, in1=h_tiles[i][:], op0=MAX, op1=ADD)
             nc.sync.dma_start(out=out_rows[i], in_=o[:])
 
-        for step in range(TILES + 4):
+        stack.enter_context(tc.manual_schedule())
+        for step in range(TILES + 6):
             if step + X_AHEAD < TILES:
                 load_x(step + X_AHEAD)
+            if 0 <= step - 5 < TILES:
+                quantise_h_2(step - 5)
+            if 0 <= step - 6 < TILES:
+                finish(step - 6)
             if 0 <= step - 3 < TILES:
-                quantise_h_2(step - 3)
+                relu_of_vector_half(step - 3)
+            if 0 <= step - 2 < TILES:
+                feature_layers(step - 2)
             if 0 <= step - 4 < TILES:
-                finish(step - 4)
-            if 0 <= step - 1 < TILES:
-                feature_layers(step - 1)
+                quantise_h(step - 4)
             if step < TILES:
                 transpose_x(step)
             if 0 <= step - 2 < TILES:
-                quantise_h(step - 2)
-            if 0 <= step - 1 < TILES:
-                relu_of_vector_half(step - 1)
-            if 0 <= step - 3 < TILES:
-                second_layer(step - 3)
+                round_h(step - 2)
+            if 0 <= step - 5 < TILES:
+                second_layer(step - 5)

@@ -38,6 +38,7 @@ def tile_dsfs_pa_t_kernel(tc, x, feat_w, feat_b, trans_w_words, trans_w_scales, 
         x_pool = stack.enter_context(tc.tile_pool(name="x_pool", bufs=X_AHEAD + 2))
         xt_pool = stack.enter_context(tc.tile_pool(name="xt_pool", bufs=3))
         h_pool = stack.enter_context(tc.tile_pool(name="h_pool", bufs=7))
+        hr_pool = stack.enter_context(tc.tile_pool(name="hr_pool", bufs=3))
         hb_pool = stack.enter_context(tc.tile_pool(name="hb_pool", bufs=3))
         q_pool = stack.enter_context(tc.tile_pool(name="q_pool", bufs=3))
         o_pool = stack.enter_context(tc.tile_pool(name="o_pool", bufs=4))
@@ -52,6 +53,7 @@ def tile_dsfs_pa_t_kernel(tc, x, feat_w, feat_b, trans_w_words, trans_w_scales, 
         hb_tiles = {}
         code_tiles = {}
         o_tiles = {}
+        hr_tiles = {}
 
         def load_x(i):
             x_sb = x_pool.tile([P, FH], BF16)
@@ -121,9 +123,9 @@ def tile_dsfs_pa_t_kernel(tc, x, feat_w, feat_b, trans_w_words, trans_w_scales, 
             hb_tiles[i] = hb
 
         def relu_of_vector_half(i):
-            cols = slice(K_PASS, FH)
-            h = h_tiles[i]
-            nc.gpsimd.tensor_scalar(out=h[:, cols], in0=h[:, cols], scalar1=float("inf"), scalar2=0.0, op0=MIN, op1=MAX)
+            hr = hr_pool.tile([P, K_PASS], F32)
+            nc.gpsimd.tensor_scalar(out=hr[:], in0=h_tiles[i][:, K_PASS:FH], scalar1=float("inf"), scalar2=0.0, op0=MIN, op1=MAX)
+            hr_tiles[i] = hr
 
         def quantise_h(i):
             ht_ps = ht_psum.tile([P, PASSES, 2, P], F32)
@@ -168,7 +170,10 @@ def tile_dsfs_pa_t_kernel(tc, x, feat_w, feat_b, trans_w_words, trans_w_scales, 
 
         def finish(i):
             o = o_tiles[i]
-            nc.vector.scalar_tensor_tensor(out=o[:], in0=o[:], scalar=0.0, in1=h_tiles[i][:], op0=MAX, op1=ADD)
+            left = slice(0, K_PASS)
+            right = slice(K_PASS, FH)
+            nc.vector.scalar_tensor_tensor(out=o[:, left], in0=o[:, left], scalar=0.0, in1=h_tiles[i][:, left], op0=MAX, op1=ADD)
+            nc.vector.scalar_tensor_tensor(out=o[:, right], in0=o[:, right], scalar=0.0, in1=hr_tiles[i][:], op0=MAX, op1=ADD)
             nc.sync.dma_start(out=out_rows[i], in_=o[:])
 
         stack.enter_context(tc.manual_schedule())

@@ -73,7 +73,8 @@ def tile_dsfs_pa_t_kernel(tc, x, feat_w, feat_b, trans_w_words, trans_w_scales, 
         nc.sync.dma_start(out=fw[:], in_=feat_w.rearrange("f e h -> e f h"))
         fb = consts.tile([P, FH], BF16)
         nc.sync.dma_start(out=fb[:], in_=feat_b.rearrange("f h -> (f h)").partition_broadcast(P))
-        load_x(1)
+        for i in range(1, X_AHEAD):
+            load_x(i)
         for quad in range(4):
             nc.sync.dma_start(
                 out=w_scales[32 * quad : 32 * quad + 4, :, :].bitcast(I32),
@@ -87,8 +88,6 @@ def tile_dsfs_pa_t_kernel(tc, x, feat_w, feat_b, trans_w_words, trans_w_scales, 
             )
         tb = consts.tile([P, FH], BF16)
         nc.sync.dma_start(out=tb[:], in_=trans_b.partition_broadcast(P))
-        for i in range(2, X_AHEAD):
-            load_x(i)
 
         def transpose_x(i):
             xt_ps = xt_psum.tile([P, F, P], BF16)
@@ -117,9 +116,13 @@ def tile_dsfs_pa_t_kernel(tc, x, feat_w, feat_b, trans_w_words, trans_w_scales, 
                 )
             nc.vector.tensor_tensor(out=h[:, right], in0=pre_right[:], in1=fb[:, right], op=ADD)
 
-        def round_h(i):
+        def round_h(i, by_vector):
             hb = hb_pool.tile([P, 2, FH // 4, 2], BF16)
-            nc.scalar.activation(out=hb[:], in_=h_tiles[i][:].rearrange("p (c u e) -> p u c e", u=2, e=2), func=RELU)
+            sorted_h = h_tiles[i][:].rearrange("p (c u e) -> p u c e", u=2, e=2)
+            if by_vector:
+                nc.vector.tensor_scalar(out=hb[:], in0=sorted_h, scalar1=0.0, scalar2=None, op0=MAX)
+            else:
+                nc.scalar.activation(out=hb[:], in_=sorted_h, func=RELU)
             hb_tiles[i] = hb
 
         def relu_of_vector_half(i):
@@ -173,8 +176,9 @@ def tile_dsfs_pa_t_kernel(tc, x, feat_w, feat_b, trans_w_words, trans_w_scales, 
             left = slice(0, K_PASS)
             right = slice(K_PASS, FH)
             nc.vector.scalar_tensor_tensor(out=o[:, left], in0=o[:, left], scalar=0.0, in1=h_tiles[i][:, left], op0=MAX, op1=ADD)
+            nc.sync.dma_start(out=out_rows[i][:, left], in_=o[:, left])
             nc.vector.scalar_tensor_tensor(out=o[:, right], in0=o[:, right], scalar=0.0, in1=hr_tiles[i][:], op0=MAX, op1=ADD)
-            nc.sync.dma_start(out=out_rows[i], in_=o[:])
+            nc.sync.dma_start(out=out_rows[i][:, right], in_=o[:, right])
 
         stack.enter_context(tc.manual_schedule())
         for step in range(TILES + 6):
@@ -193,6 +197,6 @@ def tile_dsfs_pa_t_kernel(tc, x, feat_w, feat_b, trans_w_words, trans_w_scales, 
             if step < TILES:
                 transpose_x(step)
             if 0 <= step - 2 < TILES:
-                round_h(step - 2)
+                round_h(step - 2, by_vector=(step < 5))
             if 0 <= step - 5 < TILES:
                 second_layer(step - 5)

@@ -24,6 +24,8 @@ BANK = 512
 HALVES = FH // BANK
 TILES = B // P
 X_AHEAD = 4
+VECTOR_FIRST = 4
+TENSOR_LAST = 2
 
 FLOPS = 2 * B * (F * E * H + FH * FH)
 
@@ -39,6 +41,7 @@ def tile_dsfs_pa_t_kernel(tc, x, feat_w, feat_b, trans_w_words, trans_w_scales, 
         xt_pool = stack.enter_context(tc.tile_pool(name="xt_pool", bufs=3))
         h_pool = stack.enter_context(tc.tile_pool(name="h_pool", bufs=7))
         hr_pool = stack.enter_context(tc.tile_pool(name="hr_pool", bufs=3))
+        hl_pool = stack.enter_context(tc.tile_pool(name="hl_pool", bufs=VECTOR_FIRST))
         hb_pool = stack.enter_context(tc.tile_pool(name="hb_pool", bufs=3))
         q_pool = stack.enter_context(tc.tile_pool(name="q_pool", bufs=3))
         o_pool = stack.enter_context(tc.tile_pool(name="o_pool", bufs=4))
@@ -97,24 +100,31 @@ def tile_dsfs_pa_t_kernel(tc, x, feat_w, feat_b, trans_w_words, trans_w_scales, 
             nc.scalar.copy(out=xt[:], in_=xt_ps[:])
             xt_tiles[i] = xt
 
+        def bias_on_tensor(i, g):
+            return i >= VECTOR_FIRST if g == 0 else i >= TILES - TENSOR_LAST
+
         def feature_layers(i):
             h = h_pool.tile([P, FH], F32)
             h_tiles[i] = h
-            left = slice(0, K_PASS)
-            right = slice(K_PASS, FH)
-            pre_left = pre_psum.tile([P, K_PASS], F32, name="pre_ps")
-            nc.tensor.matmul(pre_left[:], lhsT=ident_bf[:], rhs=fb[:, left], start=True, stop=False)
-            for f in range(F_PASS):
-                nc.tensor.matmul(
-                    pre_left[:, f * H : (f + 1) * H], lhsT=xt_tiles[i][:, f, :], rhs=fw[:, f, :], start=False, stop=(f == F_PASS - 1)
-                )
-            nc.scalar.activation(out=h[:, left], in_=pre_left[:], func=RELU)
-            pre_right = pre_psum.tile([P, K_PASS], F32, name="pre_ps")
-            for f in range(F_PASS, F):
-                nc.tensor.matmul(
-                    pre_right[:, (f - F_PASS) * H : (f - F_PASS + 1) * H], lhsT=xt_tiles[i][:, f, :], rhs=fw[:, f, :], start=True, stop=True
-                )
-            nc.vector.tensor_tensor(out=h[:, right], in0=pre_right[:], in1=fb[:, right], op=ADD)
+            for g in range(PASSES):
+                cols = slice(g * K_PASS, (g + 1) * K_PASS)
+                on_tensor = bias_on_tensor(i, g)
+                pre = pre_psum.tile([P, K_PASS], F32, name="pre_ps")
+                if on_tensor:
+                    nc.tensor.matmul(pre[:], lhsT=ident_bf[:], rhs=fb[:, cols], start=True, stop=False)
+                for j in range(F_PASS):
+                    f = g * F_PASS + j
+                    nc.tensor.matmul(
+                        pre[:, j * H : (j + 1) * H],
+                        lhsT=xt_tiles[i][:, f, :],
+                        rhs=fw[:, f, :],
+                        start=not on_tensor,
+                        stop=(j == F_PASS - 1) or not on_tensor,
+                    )
+                if on_tensor:
+                    nc.scalar.activation(out=h[:, cols], in_=pre[:], func=RELU)
+                else:
+                    nc.vector.tensor_tensor(out=h[:, cols], in0=pre[:], in1=fb[:, cols], op=ADD)
 
         def round_h(i, by_vector):
             hb = hb_pool.tile([P, 2, FH // 4, 2], BF16)
@@ -125,10 +135,14 @@ def tile_dsfs_pa_t_kernel(tc, x, feat_w, feat_b, trans_w_words, trans_w_scales, 
                 nc.scalar.activation(out=hb[:], in_=sorted_h, func=RELU)
             hb_tiles[i] = hb
 
-        def relu_of_vector_half(i):
-            hr = hr_pool.tile([P, K_PASS], F32)
-            nc.gpsimd.tensor_scalar(out=hr[:], in0=h_tiles[i][:, K_PASS:FH], scalar1=float("inf"), scalar2=0.0, op0=MIN, op1=MAX)
-            hr_tiles[i] = hr
+        def relu_by_gpsimd(i):
+            for g in range(PASSES):
+                if not bias_on_tensor(i, g):
+                    hr = (hl_pool if g == 0 else hr_pool).tile([P, K_PASS], F32, name="hr")
+                    nc.gpsimd.tensor_scalar(
+                        out=hr[:], in0=h_tiles[i][:, g * K_PASS : (g + 1) * K_PASS], scalar1=float("inf"), scalar2=0.0, op0=MIN, op1=MAX
+                    )
+                    hr_tiles[(i, g)] = hr
 
         def quantise_h(i):
             ht_ps = ht_psum.tile([P, PASSES, 2, P], F32)
@@ -173,12 +187,11 @@ def tile_dsfs_pa_t_kernel(tc, x, feat_w, feat_b, trans_w_words, trans_w_scales, 
 
         def finish(i):
             o = o_tiles[i]
-            left = slice(0, K_PASS)
-            right = slice(K_PASS, FH)
-            nc.vector.scalar_tensor_tensor(out=o[:, left], in0=o[:, left], scalar=0.0, in1=h_tiles[i][:, left], op0=MAX, op1=ADD)
-            nc.sync.dma_start(out=out_rows[i][:, left], in_=o[:, left])
-            nc.vector.scalar_tensor_tensor(out=o[:, right], in0=o[:, right], scalar=0.0, in1=hr_tiles[i][:], op0=MAX, op1=ADD)
-            nc.sync.dma_start(out=out_rows[i][:, right], in_=o[:, right])
+            for g in range(PASSES):
+                cols = slice(g * K_PASS, (g + 1) * K_PASS)
+                h_relu = h_tiles[i][:, cols] if bias_on_tensor(i, g) else hr_tiles[(i, g)][:]
+                nc.vector.scalar_tensor_tensor(out=o[:, cols], in0=o[:, cols], scalar=0.0, in1=h_relu, op0=MAX, op1=ADD)
+                nc.sync.dma_start(out=out_rows[i][:, cols], in_=o[:, cols])
 
         stack.enter_context(tc.manual_schedule())
         for step in range(TILES + 6):
@@ -189,7 +202,7 @@ def tile_dsfs_pa_t_kernel(tc, x, feat_w, feat_b, trans_w_words, trans_w_scales, 
             if 0 <= step - 6 < TILES:
                 finish(step - 6)
             if 0 <= step - 3 < TILES:
-                relu_of_vector_half(step - 3)
+                relu_by_gpsimd(step - 3)
             if 0 <= step - 2 < TILES:
                 feature_layers(step - 2)
             if 0 <= step - 4 < TILES:

@@ -23,7 +23,7 @@ F_PASS = K_PASS // H
 BANK = 512
 HALVES = FH // BANK
 TILES = B // P
-X_AHEAD = 4
+X_AHEAD = 5
 VECTOR_FIRST = 4
 TENSOR_LAST = 2
 
@@ -74,9 +74,10 @@ def tile_dsfs_pa_t_kernel(tc, x, feat_w, feat_b, trans_w_words, trans_w_scales, 
         load_x(0)
         fw = consts.tile([P, F, H], BF16)
         nc.sync.dma_start(out=fw[:], in_=feat_w.rearrange("f e h -> e f h"))
+        load_x(1)
         fb = consts.tile([P, FH], BF16)
         nc.sync.dma_start(out=fb[:], in_=feat_b.rearrange("f h -> (f h)").partition_broadcast(P))
-        for i in range(1, X_AHEAD):
+        for i in range(2, X_AHEAD):
             load_x(i)
         for quad in range(4):
             nc.sync.dma_start(
@@ -126,13 +127,10 @@ def tile_dsfs_pa_t_kernel(tc, x, feat_w, feat_b, trans_w_words, trans_w_scales, 
                 else:
                     nc.vector.tensor_tensor(out=h[:, cols], in0=pre[:], in1=fb[:, cols], op=ADD)
 
-        def round_h(i, by_vector):
+        def round_h(i):
             hb = hb_pool.tile([P, 2, FH // 4, 2], BF16)
             sorted_h = h_tiles[i][:].rearrange("p (c u e) -> p u c e", u=2, e=2)
-            if by_vector:
-                nc.vector.tensor_scalar(out=hb[:], in0=sorted_h, scalar1=0.0, scalar2=None, op0=MAX)
-            else:
-                nc.scalar.activation(out=hb[:], in_=sorted_h, func=RELU)
+            nc.scalar.activation(out=hb[:], in_=sorted_h, func=RELU)
             hb_tiles[i] = hb
 
         def relu_by_gpsimd(i):
@@ -210,6 +208,6 @@ def tile_dsfs_pa_t_kernel(tc, x, feat_w, feat_b, trans_w_words, trans_w_scales, 
             if step < TILES:
                 transpose_x(step)
             if 0 <= step - 2 < TILES:
-                round_h(step - 2, by_vector=(step < 5))
+                round_h(step - 2)
             if 0 <= step - 5 < TILES:
                 second_layer(step - 5)

@@ -189,7 +189,10 @@ def tile_dsfs_pa_t_kernel(tc, x, feat_w, feat_b, trans_w_words, trans_w_scales, 
                 cols = slice(g * K_PASS, (g + 1) * K_PASS)
                 h_relu = h_tiles[i][:, cols] if bias_on_tensor(i, g) else hr_tiles[(i, g)][:]
                 nc.vector.scalar_tensor_tensor(out=o[:, cols], in0=o[:, cols], scalar=0.0, in1=h_relu, op0=MAX, op1=ADD)
-                nc.sync.dma_start(out=out_rows[i][:, cols], in_=o[:, cols])
+                if i == TILES - 1:
+                    nc.sync.dma_start(out=out_rows[i][:, cols], in_=o[:, cols])
+            if i < TILES - 1:
+                nc.sync.dma_start(out=out_rows[i], in_=o[:])
 
         stack.enter_context(tc.manual_schedule())
         for step in range(TILES + 6):

@@ -91,7 +91,6 @@ def tile_dsfs_pa_t_kernel(tc, x, feat_w, feat_b, trans_w_words, trans_w_scales, 
                 in_=trans_w_words[g].rearrange("p n t -> p (n t)").bitcast(I32),
             )
         tb = consts.tile([P, FH], BF16)
-        nc.sync.dma_start(out=tb[:], in_=trans_b.partition_broadcast(P))
 
         def transpose_x(i):
             xt_ps = xt_psum.tile([P, F, P], BF16)
@@ -210,6 +209,8 @@ def tile_dsfs_pa_t_kernel(tc, x, feat_w, feat_b, trans_w_words, trans_w_scales, 
                 quantise_h(step - 4)
             if step < TILES:
                 transpose_x(step)
+            if step == 1:
+                nc.scalar.dma_start(out=tb[:], in_=trans_b.partition_broadcast(P))
             if 0 <= step - 2 < TILES:
                 round_h(step - 2)
             if 0 <= step - 5 < TILES:

@@ -68,17 +68,21 @@ def tile_dsfs_pa_t_kernel(tc, x, feat_w, feat_b, trans_w_words, trans_w_scales, 
         ident_f32 = consts.tile([P, P], F32)
         make_identity(nc, ident_f32[:])
 
+        fb_row = consts.tile([P, FH], BF16)
+        nc.vector.memset(fb_row[:], 0.0)
+        nc.scalar.dma_start(out=fb_row[0:1, :], in_=feat_b.rearrange("(o f) h -> o (f h)", o=1))
+        ones = consts.tile([P, P], BF16)
+        nc.vector.memset(ones[:], 1.0)
+
         w_scales = consts.tile([P, PASSES, FH], U8, align_bytes=64)
         nc.vector.memset(w_scales[:].bitcast(I32), 0)
 
         load_x(0)
         fw = consts.tile([P, F, H], BF16)
         nc.sync.dma_start(out=fw[:], in_=feat_w.rearrange("f e h -> e f h"))
-        load_x(1)
-        fb = consts.tile([P, FH], BF16)
-        nc.sync.dma_start(out=fb[:], in_=feat_b.rearrange("f h -> (f h)").partition_broadcast(P))
-        for i in range(2, X_AHEAD):
+        for i in range(1, X_AHEAD):
             load_x(i)
+        fb = consts.tile([P, FH], BF16)
         for quad in range(4):
             nc.sync.dma_start(
                 out=w_scales[32 * quad : 32 * quad + 4, :, :].bitcast(I32),
@@ -91,6 +95,13 @@ def tile_dsfs_pa_t_kernel(tc, x, feat_w, feat_b, trans_w_words, trans_w_scales, 
                 in_=trans_w_words[g].rearrange("p n t -> p (n t)").bitcast(I32),
             )
         tb = consts.tile([P, FH], BF16)
+
+        def spread_feat_b():
+            for g in range(PASSES):
+                cols = slice(g * K_PASS, (g + 1) * K_PASS)
+                pre = pre_psum.tile([P, K_PASS], F32, name="pre_ps")
+                nc.tensor.matmul(pre[:], lhsT=ones[:], rhs=fb_row[:, cols], start=True, stop=True)
+                nc.vector.tensor_copy(out=fb[:, cols], in_=pre[:])
 
         def transpose_x(i):
             xt_ps = xt_psum.tile([P, F, P], BF16)
@@ -209,6 +220,8 @@ def tile_dsfs_pa_t_kernel(tc, x, feat_w, feat_b, trans_w_words, trans_w_scales, 
                 quantise_h(step - 4)
             if step < TILES:
                 transpose_x(step)
+            if step == 0:
+                spread_feat_b()
             if step == 1:
                 nc.scalar.dma_start(out=tb[:], in_=trans_b.partition_broadcast(P))
             if 0 <= step - 2 < TILES:

@@ -25,6 +25,7 @@ HALVES = FH // BANK
 TILES = B // P
 X_AHEAD = 5
 VECTOR_FIRST = 4
+LAST_PIECE = 256
 TENSOR_LAST = 2
 
 FLOPS = 2 * B * (F * E * H + FH * FH)
@@ -69,8 +70,8 @@ def tile_dsfs_pa_t_kernel(tc, x, feat_w, feat_b, trans_w_words, trans_w_scales, 
         make_identity(nc, ident_f32[:])
 
         fb_row = consts.tile([P, FH], BF16)
-        nc.vector.memset(fb_row[:], 0.0)
-        nc.scalar.dma_start(out=fb_row[0:1, :], in_=feat_b.rearrange("(o f) h -> o (f h)", o=1))
+        nc.scalar.dma_start(out=fb_row[P - 1 : P, :], in_=feat_b.rearrange("(o f) h -> o (f h)", o=1))
+        nc.vector.memset(fb_row[0 : P - 1, :].bitcast(I32), 0)
         ones = consts.tile([P, P], BF16)
         nc.vector.memset(ones[:], 1.0)
 
@@ -101,7 +102,10 @@ def tile_dsfs_pa_t_kernel(tc, x, feat_w, feat_b, trans_w_words, trans_w_scales, 
                 cols = slice(g * K_PASS, (g + 1) * K_PASS)
                 pre = pre_psum.tile([P, K_PASS], F32, name="pre_ps")
                 nc.tensor.matmul(pre[:], lhsT=ones[:], rhs=fb_row[:, cols], start=True, stop=True)
-                nc.vector.tensor_copy(out=fb[:, cols], in_=pre[:])
+                if g == 0:
+                    nc.vector.tensor_copy(out=fb[:, cols], in_=pre[:])
+                else:
+                    nc.scalar.copy(out=fb[:, cols], in_=pre[:])
 
         def transpose_x(i):
             xt_ps = xt_psum.tile([P, F, P], BF16)
@@ -195,13 +199,16 @@ def tile_dsfs_pa_t_kernel(tc, x, feat_w, feat_b, trans_w_words, trans_w_scales, 
 
         def finish(i):
             o = o_tiles[i]
-            for g in range(PASSES):
-                cols = slice(g * K_PASS, (g + 1) * K_PASS)
-                h_relu = h_tiles[i][:, cols] if bias_on_tensor(i, g) else hr_tiles[(i, g)][:]
-                nc.vector.scalar_tensor_tensor(out=o[:, cols], in0=o[:, cols], scalar=0.0, in1=h_relu, op0=MAX, op1=ADD)
-                if i == TILES - 1:
+            if i == TILES - 1:
+                for c0 in range(0, FH, LAST_PIECE):
+                    cols = slice(c0, c0 + LAST_PIECE)
+                    nc.vector.scalar_tensor_tensor(out=o[:, cols], in0=o[:, cols], scalar=0.0, in1=h_tiles[i][:, cols], op0=MAX, op1=ADD)
                     nc.sync.dma_start(out=out_rows[i][:, cols], in_=o[:, cols])
-            if i < TILES - 1:
+            else:
+                for g in range(PASSES):
+                    cols = slice(g * K_PASS, (g + 1) * K_PASS)
+                    h_relu = h_tiles[i][:, cols] if bias_on_tensor(i, g) else hr_tiles[(i, g)][:]
+                    nc.vector.scalar_tensor_tensor(out=o[:, cols], in0=o[:, cols], scalar=0.0, in1=h_relu, op0=MAX, op1=ADD)
                 nc.sync.dma_start(out=out_rows[i], in_=o[:])
 
         stack.enter_context(tc.manual_schedule())

@@ -26,6 +26,7 @@ TILES = B // P
 X_AHEAD = 5
 VECTOR_FIRST = 4
 LAST_PIECE = 256
+G_COLS = 128
 TENSOR_LAST = 2
 
 FLOPS = 2 * B * (F * E * H + FH * FH)
@@ -45,7 +46,7 @@ def tile_dsfs_pa_t_kernel(tc, x, feat_w, feat_b, trans_w_words, trans_w_scales, 
         hl_pool = stack.enter_context(tc.tile_pool(name="hl_pool", bufs=VECTOR_FIRST))
         hb_pool = stack.enter_context(tc.tile_pool(name="hb_pool", bufs=3))
         q_pool = stack.enter_context(tc.tile_pool(name="q_pool", bufs=3))
-        o_pool = stack.enter_context(tc.tile_pool(name="o_pool", bufs=4))
+        o_pool = stack.enter_context(tc.tile_pool(name="o_pool", bufs=5))
         xt_psum = stack.enter_context(tc.psum_pool(name="xt_psum", bufs=2))
         pre_psum = stack.enter_context(tc.psum_pool(name="pre_psum", bufs=2))
         ht_psum = stack.enter_context(tc.psum_pool(name="ht_psum", bufs=2))
@@ -206,10 +207,24 @@ def tile_dsfs_pa_t_kernel(tc, x, feat_w, feat_b, trans_w_words, trans_w_scales, 
                     nc.sync.dma_start(out=out_rows[i][:, cols], in_=o[:, cols])
             else:
                 for g in range(PASSES):
-                    cols = slice(g * K_PASS, (g + 1) * K_PASS)
-                    h_relu = h_tiles[i][:, cols] if bias_on_tensor(i, g) else hr_tiles[(i, g)][:]
+                    end = K_PASS - g_cols(i) if g == PASSES - 1 else K_PASS
+                    cols = slice(g * K_PASS, g * K_PASS + end)
+                    h_relu = h_tiles[i][:, cols] if bias_on_tensor(i, g) else hr_tiles[(i, g)][:, 0:end]
                     nc.vector.scalar_tensor_tensor(out=o[:, cols], in0=o[:, cols], scalar=0.0, in1=h_relu, op0=MAX, op1=ADD)
+                finish_by_gpsimd(i)
                 nc.sync.dma_start(out=out_rows[i], in_=o[:])
+
+        def g_cols(i):
+            return 0 if i >= TILES - TENSOR_LAST else G_COLS
+
+        def finish_by_gpsimd(i):
+            n = g_cols(i)
+            if n:
+                o = o_tiles[i]
+                hr = hr_tiles[(i, PASSES - 1)]
+                cols = slice(FH - n, FH)
+                nc.gpsimd.tensor_scalar(out=hr[:, 0:n], in0=o[:, cols], scalar1=float("inf"), scalar2=0.0, op0=MIN, op1=MAX)
+                nc.gpsimd.tensor_tensor(out=o[:, cols], in0=hr[:, 0:n], in1=hr[:, K_PASS - n : K_PASS], op=ADD)
 
         stack.enter_context(tc.manual_schedule())
         for step in range(TILES + 6):

from contextlib import ExitStack

import concourse.mybir as mybir
from concourse.masks import make_identity

FP8X4 = mybir.dt.float8_e4m3fn_x4
BF16 = mybir.dt.bfloat16
F32 = mybir.dt.float32
I32 = mybir.dt.int32
U32 = mybir.dt.uint32
U8 = mybir.dt.uint8
ADD = mybir.AluOpType.add
MAX = mybir.AluOpType.max
MIN = mybir.AluOpType.min
RELU = mybir.ActivationFunctionType.Relu

P = 128
B, F, E, H = 4096, 8, 128, 128
FH = F * H
K_PASS = 4 * P
PASSES = FH // K_PASS
F_PASS = K_PASS // H
BANK = 512
HALVES = FH // BANK
TILES = B // P
X_AHEAD = 5
VECTOR_FIRST = 4
LAST_PIECE = 256
G_COLS = 128
TENSOR_LAST = 2

FLOPS = 2 * B * (F * E * H + FH * FH)


def tile_dsfs_pa_t_kernel(tc, x, feat_w, feat_b, trans_w_words, trans_w_scales, trans_b, out):
    nc = tc.nc
    x_rows = x.rearrange("(i p) f e -> i p (f e)", p=P)
    out_rows = out.rearrange("(i p) n -> i p n", p=P)

    with ExitStack() as stack:
        consts = stack.enter_context(tc.tile_pool(name="consts", bufs=1))
        x_pool = stack.enter_context(tc.tile_pool(name="x_pool", bufs=X_AHEAD + 2))
        xt_pool = stack.enter_context(tc.tile_pool(name="xt_pool", bufs=3))
        h_pool = stack.enter_context(tc.tile_pool(name="h_pool", bufs=7))
        hr_pool = stack.enter_context(tc.tile_pool(name="hr_pool", bufs=3))
        hl_pool = stack.enter_context(tc.tile_pool(name="hl_pool", bufs=VECTOR_FIRST))
        hb_pool = stack.enter_context(tc.tile_pool(name="hb_pool", bufs=3))
        q_pool = stack.enter_context(tc.tile_pool(name="q_pool", bufs=3))
        o_pool = stack.enter_context(tc.tile_pool(name="o_pool", bufs=5))
        xt_psum = stack.enter_context(tc.psum_pool(name="xt_psum", bufs=2))
        pre_psum = stack.enter_context(tc.psum_pool(name="pre_psum", bufs=2))
        ht_psum = stack.enter_context(tc.psum_pool(name="ht_psum", bufs=2))
        acc_psum = stack.enter_context(tc.psum_pool(name="acc_psum", bufs=2))

        x_tiles = {}
        xt_tiles = {}
        h_tiles = {}
        hb_tiles = {}
        code_tiles = {}
        o_tiles = {}
        hr_tiles = {}

        def load_x(i):
            x_sb = x_pool.tile([P, FH], BF16)
            nc.sync.dma_start(out=x_sb[:], in_=x_rows[i])
            x_tiles[i] = x_sb

        ident_bf = consts.tile([P, P], BF16)
        make_identity(nc, ident_bf[:])
        ident_f32 = consts.tile([P, P], F32)
        make_identity(nc, ident_f32[:])

        fb_row = consts.tile([P, FH], BF16)
        nc.scalar.dma_start(out=fb_row[P - 1 : P, :], in_=feat_b.rearrange("(o f) h -> o (f h)", o=1))
        nc.vector.memset(fb_row[0 : P - 1, :].bitcast(I32), 0)
        ones = consts.tile([P, P], BF16)
        nc.vector.memset(ones[:], 1.0)

        w_scales = consts.tile([P, PASSES, FH], U8, align_bytes=64)
        nc.vector.memset(w_scales[:].bitcast(I32), 0)

        load_x(0)
        fw = consts.tile([P, F, H], BF16)
        nc.sync.dma_start(out=fw[:], in_=feat_w.rearrange("f e h -> e f h"))
        for i in range(1, X_AHEAD):
            load_x(i)
        fb = consts.tile([P, FH], BF16)
        for quad in range(4):
            nc.sync.dma_start(
                out=w_scales[32 * quad : 32 * quad + 4, :, :].bitcast(I32),
                in_=trans_w_scales[:, 4 * quad : 4 * quad + 4, :].rearrange("g r n -> r g n").bitcast(I32),
            )
        w_codes = consts.tile([P, PASSES, FH], U32, align_bytes=64)
        for g in range(PASSES):
            nc.sync.dma_start(
                out=w_codes[:, g, :].bitcast(I32),
                in_=trans_w_words[g].rearrange("p n t -> p (n t)").bitcast(I32),
            )
        tb = consts.tile([P, FH], BF16)

        def spread_feat_b():
            for g in range(PASSES):
                cols = slice(g * K_PASS, (g + 1) * K_PASS)
                pre = pre_psum.tile([P, K_PASS], F32, name="pre_ps")
                nc.tensor.matmul(pre[:], lhsT=ones[:], rhs=fb_row[:, cols], start=True, stop=True)
                if g == 0:
                    nc.vector.tensor_copy(out=fb[:, cols], in_=pre[:])
                else:
                    nc.scalar.copy(out=fb[:, cols], in_=pre[:])

        def transpose_x(i):
            xt_ps = xt_psum.tile([P, F, P], BF16)
            for f in range(F):
                nc.tensor.transpose(xt_ps[:, f, :], x_tiles[i][:, f * E : (f + 1) * E], ident_bf[:])
            xt = xt_pool.tile([P, F, P], BF16)
            nc.scalar.copy(out=xt[:], in_=xt_ps[:])
            xt_tiles[i] = xt

        def bias_on_tensor(i, g):
            return i >= VECTOR_FIRST if g == 0 else i >= TILES - TENSOR_LAST

        def feature_layers(i):
            h = h_pool.tile([P, FH], F32)
            h_tiles[i] = h
            for g in range(PASSES):
                cols = slice(g * K_PASS, (g + 1) * K_PASS)
                on_tensor = bias_on_tensor(i, g)
                pre = pre_psum.tile([P, K_PASS], F32, name="pre_ps")
                if on_tensor:
                    nc.tensor.matmul(pre[:], lhsT=ident_bf[:], rhs=fb[:, cols], start=True, stop=False)
                for j in range(F_PASS):
                    f = g * F_PASS + j
                    nc.tensor.matmul(
                        pre[:, j * H : (j + 1) * H],
                        lhsT=xt_tiles[i][:, f, :],
                        rhs=fw[:, f, :],
                        start=not on_tensor,
                        stop=(j == F_PASS - 1) or not on_tensor,
                    )
                if on_tensor:
                    nc.scalar.activation(out=h[:, cols], in_=pre[:], func=RELU)
                else:
                    nc.vector.tensor_tensor(out=h[:, cols], in0=pre[:], in1=fb[:, cols], op=ADD)

        def round_h(i):
            hb = hb_pool.tile([P, 2, FH // 4, 2], BF16)
            sorted_h = h_tiles[i][:].rearrange("p (c u e) -> p u c e", u=2, e=2)
            nc.scalar.activation(out=hb[:], in_=sorted_h, func=RELU)
            hb_tiles[i] = hb

        def relu_by_gpsimd(i):
            for g in range(PASSES):
                if not bias_on_tensor(i, g):
                    hr = (hl_pool if g == 0 else hr_pool).tile([P, K_PASS], F32, name="hr")
                    nc.gpsimd.tensor_scalar(
                        out=hr[:], in0=h_tiles[i][:, g * K_PASS : (g + 1) * K_PASS], scalar1=float("inf"), scalar2=0.0, op0=MIN, op1=MAX
                    )
                    hr_tiles[(i, g)] = hr

        def quantise_h(i):
            ht_ps = ht_psum.tile([P, PASSES, 2, P], F32)
            hb_words = hb_tiles[i][:].rearrange("p u c e -> p u (c e)").bitcast(F32)
            for g in range(PASSES):
                for u in range(2):
                    nc.tensor.transpose(ht_ps[:, g, u, :], hb_words[:, u, g * P : (g + 1) * P], ident_f32[:])
            grouped = q_pool.tile([P, PASSES, K_PASS], BF16, align_bytes=64)
            nc.scalar.copy(
                out=grouped[:].bitcast(F32).rearrange("p g (r u) -> p g r u", u=2),
                in_=ht_ps[:].rearrange("p g u r -> p g r u"),
            )
            h_codes = q_pool.tile([P, PASSES * P], U32, align_bytes=64)
            h_scales = q_pool.tile([P, PASSES * P], U8, align_bytes=64)
            code_tiles[i] = (grouped, h_codes, h_scales)

        def quantise_h_2(i):
            grouped, h_codes, h_scales = code_tiles[i]
            nc.vector.quantize_mx(
                out=h_codes[:].bitcast(FP8X4), scales=h_scales[:], in_=grouped[:].rearrange("p g c -> p (g c)")
            )

        def second_layer(i):
            grouped, h_codes, h_scales = code_tiles[i]
            o = o_pool.tile([P, FH], F32)
            for half in range(HALVES):
                cols = slice(half * BANK, (half + 1) * BANK)
                acc = acc_psum.tile([P, BANK], F32)
                for g in range(PASSES):
                    rows = slice(g * P, (g + 1) * P)
                    nc.tensor.matmul_mx(
                        out=acc[:],
                        lhsT=h_codes[:, rows].bitcast(FP8X4),
                        lhsT_scale=h_scales[:, rows],
                        rhs=w_codes[:, g, cols].bitcast(FP8X4),
                        rhs_scale=w_scales[:, g, cols],
                        start=(g == 0),
                        stop=(g == PASSES - 1),
                    )
                nc.vector.tensor_tensor(out=o[:, cols], in0=acc[:], in1=tb[:, cols], op=ADD)
            o_tiles[i] = o

        def finish(i):
            o = o_tiles[i]
            if i == TILES - 1:
                for c0 in range(0, FH, LAST_PIECE):
                    cols = slice(c0, c0 + LAST_PIECE)
                    nc.vector.scalar_tensor_tensor(out=o[:, cols], in0=o[:, cols], scalar=0.0, in1=h_tiles[i][:, cols], op0=MAX, op1=ADD)
                    nc.sync.dma_start(out=out_rows[i][:, cols], in_=o[:, cols])
            else:
                for g in range(PASSES):
                    end = K_PASS - g_cols(i) if g == PASSES - 1 else K_PASS
                    cols = slice(g * K_PASS, g * K_PASS + end)
                    h_relu = h_tiles[i][:, cols] if bias_on_tensor(i, g) else hr_tiles[(i, g)][:, 0:end]
                    nc.vector.scalar_tensor_tensor(out=o[:, cols], in0=o[:, cols], scalar=0.0, in1=h_relu, op0=MAX, op1=ADD)
                finish_by_gpsimd(i)
                nc.sync.dma_start(out=out_rows[i], in_=o[:])

        def g_cols(i):
            return 0 if i >= TILES - TENSOR_LAST else G_COLS

        def finish_by_gpsimd(i):
            n = g_cols(i)
            if n:
                o = o_tiles[i]
                hr = hr_tiles[(i, PASSES - 1)]
                cols = slice(FH - n, FH)
                nc.gpsimd.tensor_scalar(out=hr[:, 0:n], in0=o[:, cols], scalar1=float("inf"), scalar2=0.0, op0=MIN, op1=MAX)
                nc.gpsimd.tensor_tensor(out=o[:, cols], in0=hr[:, 0:n], in1=hr[:, K_PASS - n : K_PASS], op=ADD)

        stack.enter_context(tc.manual_schedule())
        for step in range(TILES + 6):
            if step + X_AHEAD < TILES:
                load_x(step + X_AHEAD)
            if 0 <= step - 5 < TILES:
                quantise_h_2(step - 5)
            if 0 <= step - 6 < TILES:
                finish(step - 6)
            if 0 <= step - 3 < TILES:
                relu_by_gpsimd(step - 3)
            if 0 <= step - 2 < TILES:
                feature_layers(step - 2)
            if 0 <= step - 4 < TILES:
                quantise_h(step - 4)
            if step < TILES:
                transpose_x(step)
            if step == 0:
                spread_feat_b()
            if step == 1:
                nc.scalar.dma_start(out=tb[:], in_=trans_b.partition_broadcast(P))
            if 0 <= step - 2 < TILES:
                round_h(step - 2)
            if 0 <= step - 5 < TILES:
                second_layer(step - 5)
